import numpy as np
import ml_dtypes


def mxq(x, axis, fmt="e4m3"):
    dtype, down = {"e4m3": (ml_dtypes.float8_e4m3fn, 7), "e5m2": (ml_dtypes.float8_e5m2, 14)}[fmt]
    v = np.moveaxis(np.asarray(x, np.float32).astype(ml_dtypes.bfloat16).astype(np.float64), axis, -1)
    blocks = v.reshape(v.shape[:-1] + (-1, 32))
    amax = np.abs(blocks).max(-1, keepdims=True)
    byte = np.maximum(np.where(amax > 0, np.frexp(amax)[1] - 1 + 127, 0) - down, 1)
    scale = np.exp2(byte - 127.0)
    codes = (blocks / scale).astype(np.float32).astype(dtype).astype(np.float64)
    return np.moveaxis((codes * scale).reshape(v.shape), -1, axis)


WIDE = False


def mx_kscale(k):
    if not WIDE:
        return np.ones(k)
    levels = np.array([10, -10, 5, -5, 0])
    a = np.random.permutation(np.resize(levels, k // 512 * 4)).reshape(k // 512, 4)
    idx = np.arange(k)
    return np.exp2(a[idx // 512, idx % 128 // 32])


BF16 = ml_dtypes.bfloat16


def bf(x):
    return np.asarray(x, np.float32).astype(BF16)


def f64(x):
    return np.asarray(x).astype(np.float64)


E2M1 = np.array([0.0, 0.5, 1.0, 1.5, 2.0, 3.0, 4.0, 6.0, -0.0, -0.5, -1.0, -1.5, -2.0, -3.0, -4.0, -6.0])


def pack_weight(w, fmt):
    k, n = w.shape
    w = f64(bf(w)).reshape(k // 32, 32, n)
    amax = np.abs(w).max(1)
    if fmt == "e4m3":
        byte = np.frexp(amax)[1] - 1 + 127 - 7
    else:
        mant, ex = np.frexp(amax / 6.0)
        byte = np.where(mant > 0.5, ex, ex - 1) + 127
    byte = np.clip(np.where(amax > 0, byte, 1), 1, 254)
    scaled = (w * np.exp2(127.0 - byte)[:, None, :]).reshape(k, n).astype(np.float32)
    by_word = np.ascontiguousarray(scaled.reshape(k // 512, 128, 4, n).transpose(0, 1, 3, 2))
    if fmt == "e4m3":
        words = by_word.astype(ml_dtypes.float8_e4m3fn).view(np.uint8)
    else:
        c = by_word.astype(ml_dtypes.float4_e2m1fn).view(np.uint8) & 0xF
        words = c[..., 0::2] | (c[..., 1::2] << 4)
    return np.ascontiguousarray(words), np.ascontiguousarray(byte.astype(np.uint8).reshape(k // 512, 16, n))


def unpack_weight(words, scales, fmt):
    g, p, n, _ = words.shape
    if fmt == "e4m3":
        vals = np.ascontiguousarray(words).view(ml_dtypes.float8_e4m3fn).astype(np.float64)
    else:
        nib = np.empty((g, p, n, 4), np.uint8)
        nib[..., 0::2] = words & 0xF
        nib[..., 1::2] = words >> 4
        vals = E2M1[nib]
    vals = vals * np.repeat(np.exp2(scales.astype(np.float64) - 127.0), 8, axis=1)[..., None]
    return vals.transpose(0, 1, 3, 2).reshape(g * 512, n)


B, S, E, H, D = 2, 64, 16384, 8, 64
NH = 2 * H
P = NH * D
BASE = 10000.0
FMT = "e4m3"


def rotary(t):
    inv_freq = 1.0 / BASE ** (np.arange(0, D, 2) / D)
    freqs = np.repeat(np.arange(S)[:, None] * inv_freq[None, :], 2, axis=-1)
    cos = np.cos(freqs)[None, :, None, :]
    sin = np.sin(freqs)[None, :, None, :]
    x = t.reshape(t.shape[:-1] + (D // 2, 2))
    x1, x2 = x[..., 0], x[..., 1]
    rot = np.stack([-x2, x1], axis=-1).reshape(t.shape)
    return t * cos + rot * sin


def setup_inputs():
    s = mx_kscale(E)
    x = bf(np.random.standard_normal((B, S, E)) * s)
    Wq_words, Wq_scales = pack_weight(np.random.standard_normal((E, P)) / np.sqrt(E) / s[:, None], FMT)
    Wk_words, Wk_scales = pack_weight(np.random.standard_normal((E, P)) / np.sqrt(E) / s[:, None], FMT)
    return {'x': x,
            'Wq_words': Wq_words, 'Wq_scales': Wq_scales,
            'Wk_words': Wk_words, 'Wk_scales': Wk_scales}


def reference(x, Wq_words, Wq_scales, Wk_words, Wk_scales):
    xq = mxq(f64(x), 2, 'e4m3')
    q = (xq @ unpack_weight(Wq_words, Wq_scales, FMT)).reshape(B, S, NH, D)
    k = (xq @ unpack_weight(Wk_words, Wk_scales, FMT)).reshape(B, S, NH, D)
    return rotary(q), rotary(k)

@@ -1,0 +1,244 @@
+import math
+from contextlib import ExitStack
+
+import concourse.mybir as mybir
+from concourse.masks import make_identity
+
+F32 = mybir.dt.float32
+BF16 = mybir.dt.bfloat16
+I32 = mybir.dt.int32
+U32 = mybir.dt.uint32
+U8 = mybir.dt.uint8
+FP8X4 = mybir.dt.float8_e4m3fn_x4
+ALU = mybir.AluOpType
+ACT = mybir.ActivationFunctionType
+
+P = 128
+POSITIONS = 64
+E = 16384
+HEAD_DIM = 64
+PAIRS = HEAD_DIM // 2
+DOUBLINGS = 5
+N = 1024
+ROPE_BASE = 10000.0
+
+PACK = 4
+K_PASS = P * PACK
+GROUPS = E // K_PASS
+BANK = 512
+BANKS_PER_WEIGHT = N // BANK
+HEADS_PER_BANK = BANK // HEAD_DIM
+
+PLANES_PER_TILE = 4
+QUADRANT = 32
+ROWS_PER_QUADRANT = 4
+
+X_CHUNK_GROUPS = 8
+X_CHUNKS = GROUPS // X_CHUNK_GROUPS
+WORDS_PER_GROUP = K_PASS // 2
+GROUPS_PER_BANK = 2
+
+W_CHUNK_GROUPS = 2
+W_CHUNKS = GROUPS // W_CHUNK_GROUPS
+W_BUFFERS = 8
+
+ROUND_MAGIC = 1.5 * 2.0**23
+TWO_PI_HIGH = 6.28125
+TWO_PI_LOW = 2.0 * math.pi - TWO_PI_HIGH
+
+FLOPS = 2 * P * E * 2 * N
+
+
+def quantise_x(nc, pools, x_rows, identity, x_codes, x_scales):
+    for c in range(X_CHUNKS):
+        x_chunk = pools["x"].tile([P, X_CHUNK_GROUPS * K_PASS], BF16, name="x_chunk")
+        columns = slice(c * X_CHUNK_GROUPS * K_PASS, (c + 1) * X_CHUNK_GROUPS * K_PASS)
+        nc.sync.dma_start(out=x_chunk[:], in_=x_rows[:, columns])
+        x_words = x_chunk[:].bitcast(F32)
+
+        grouped = pools["grouped"].tile(
+            [P, X_CHUNK_GROUPS * K_PASS], BF16, name="grouped", align_bytes=64
+        )
+        grouped_words = grouped[:].bitcast(F32)
+        for b in range(X_CHUNK_GROUPS // GROUPS_PER_BANK):
+            turned = pools["turned"].tile([P, GROUPS_PER_BANK * 2, P], F32, name="turned")
+            for i in range(GROUPS_PER_BANK):
+                first = (b * GROUPS_PER_BANK + i) * WORDS_PER_GROUP
+                for u in range(2):
+                    nc.tensor.transpose(
+                        turned[:, 2 * i + u, :],
+                        x_words[:, first + u : first + WORDS_PER_GROUP : 2],
+                        identity[:],
+                    )
+            copy = nc.vector.tensor_copy if b % 2 == 0 else nc.scalar.copy
+            copy(
+                out=grouped_words[:, b * BANK : (b + 1) * BANK].rearrange(
+                    "p (g m u) -> p g m u", g=GROUPS_PER_BANK, u=2
+                ),
+                in_=turned[:].rearrange("p (g u) m -> p g m u", u=2),
+            )
+        groups = slice(c * X_CHUNK_GROUPS, (c + 1) * X_CHUNK_GROUPS)
+        nc.vector.quantize_mx(
+            out=x_codes[:, groups, :].rearrange("p g m -> p (g m)").bitcast(FP8X4),
+            scales=x_scales[:, groups, :].rearrange("p g m -> p (g m)"),
+            in_=grouped[:],
+        )
+
+
+def load_scale_planes(nc, planes, scales):
+    for j in range(GROUPS // PLANES_PER_TILE):
+        for quadrant in range(P // QUADRANT):
+            first = quadrant * QUADRANT
+            rows = slice(quadrant * ROWS_PER_QUADRANT, (quadrant + 1) * ROWS_PER_QUADRANT)
+            nc.sync.dma_start(
+                out=planes[first : first + PLANES_PER_TILE * ROWS_PER_QUADRANT, j, :].bitcast(I32),
+                in_=scales[j * PLANES_PER_TILE : (j + 1) * PLANES_PER_TILE, rows, :].bitcast(I32),
+            )
+
+
+def project(nc, pools, words, planes, x_codes, x_scales, sums):
+    words_by_partition = words.rearrange("g p n t -> p g (n t)")
+    for c in range(W_CHUNKS):
+        w_chunk = pools["w"].tile([P, W_CHUNK_GROUPS, N], U32, name="w_chunk", align_bytes=64)
+        groups = slice(c * W_CHUNK_GROUPS, (c + 1) * W_CHUNK_GROUPS)
+        nc.sync.dma_start(
+            out=w_chunk[:].bitcast(I32), in_=words_by_partition[:, groups, :].bitcast(I32)
+        )
+        for bank in range(BANKS_PER_WEIGHT):
+            columns = slice(bank * BANK, (bank + 1) * BANK)
+            for i in range(W_CHUNK_GROUPS):
+                g = c * W_CHUNK_GROUPS + i
+                plane_offset = ROWS_PER_QUADRANT * (g % PLANES_PER_TILE)
+                nc.tensor.matmul_mx(
+                    out=sums[bank][:],
+                    lhsT=x_codes[:, g, :].bitcast(FP8X4),
+                    lhsT_scale=x_scales[:, g, :],
+                    rhs=w_chunk[:, i, columns].bitcast(FP8X4),
+                    rhs_scale=planes[plane_offset:P, g // PLANES_PER_TILE, columns],
+                    start=(g == 0),
+                    stop=(g == GROUPS - 1),
+                )
+
+
+def build_rope_tables(nc, consts):
+    position_int = consts.tile([P, 1], I32, name="position_int")
+    nc.gpsimd.iota(position_int[:], pattern=[[1, 1]], base=0, channel_multiplier=1)
+    nc.vector.tensor_single_scalar(
+        out=position_int[:], in_=position_int[:], scalar=POSITIONS - 1, op=ALU.bitwise_and
+    )
+    position = consts.tile([P, 1], F32, name="position")
+    nc.vector.tensor_copy(out=position[:], in_=position_int[:])
+
+    frequency = consts.tile([P, PAIRS], F32, name="frequency")
+    nc.vector.memset(frequency[:, 0:1], 1.0)
+    for doubling in range(DOUBLINGS):
+        width = 2**doubling
+        nc.vector.tensor_scalar_mul(
+            out=frequency[:, width : 2 * width],
+            in0=frequency[:, 0:width],
+            scalar1=ROPE_BASE ** (-2.0 * width / HEAD_DIM),
+        )
+
+    angle = consts.tile([P, 2, PAIRS], F32, name="angle")
+    nc.vector.tensor_scalar_mul(out=angle[:, 0, :], in0=frequency[:], scalar1=position[:, 0:1])
+    nc.vector.tensor_scalar_add(out=angle[:, 1, :], in0=angle[:, 0, :], scalar1=math.pi / 2.0)
+
+    turns = consts.tile([P, 2, PAIRS], F32, name="turns")
+    nc.vector.tensor_scalar(
+        out=turns[:],
+        in0=angle[:],
+        scalar1=1.0 / (2.0 * math.pi),
+        scalar2=ROUND_MAGIC,
+        op0=ALU.mult,
+        op1=ALU.add,
+    )
+    nc.vector.tensor_scalar_sub(out=turns[:], in0=turns[:], scalar1=ROUND_MAGIC)
+    for part in (TWO_PI_HIGH, TWO_PI_LOW):
+        nc.vector.scalar_tensor_tensor(
+            out=angle[:], in0=turns[:], scalar=-part, in1=angle[:], op0=ALU.mult, op1=ALU.add
+        )
+    sin_cos = consts.tile([P, 2, PAIRS], F32, name="sin_cos")
+    nc.scalar.activation(out=sin_cos[:], in_=angle[:], func=ACT.Sin)
+
+    cos = consts.tile([P, PAIRS, 2], F32, name="cos")
+    nc.vector.tensor_copy(out=cos[:], in_=sin_cos[:, 1, :].unsqueeze(2).to_broadcast([P, PAIRS, 2]))
+    minus_sin = consts.tile([P, PAIRS], F32, name="minus_sin")
+    nc.vector.tensor_scalar_mul(out=minus_sin[:], in0=sin_cos[:, 0, :], scalar1=-1.0)
+    return cos[:].rearrange("p j e -> p (j e)"), sin_cos[:, 0, :], minus_sin[:]
+
+
+def rotate_and_store(nc, pools, bank_sums, tables, out_columns, queue):
+    cos, sin, minus_sin = tables
+    by_head = [P, HEADS_PER_BANK, HEAD_DIM]
+    by_pair = [P, HEADS_PER_BANK, PAIRS]
+
+    cos_part = pools["rope"].tile(by_head, F32, name="cos_part")
+    nc.vector.tensor_mul(
+        out=cos_part[:],
+        in0=bank_sums[:].rearrange("p (h d) -> p h d", d=HEAD_DIM),
+        in1=cos.unsqueeze(1).to_broadcast(by_head),
+    )
+    partners = bank_sums[:].rearrange("p (h j e) -> p e h j", j=PAIRS, e=2)
+    sin_part = pools["rope"].tile([P, 2, HEADS_PER_BANK, PAIRS], F32, name="sin_part")
+    nc.vector.tensor_mul(
+        out=sin_part[:, 0], in0=partners[:, 1], in1=minus_sin.unsqueeze(1).to_broadcast(by_pair)
+    )
+    nc.vector.tensor_mul(
+        out=sin_part[:, 1], in0=partners[:, 0], in1=sin.unsqueeze(1).to_broadcast(by_pair)
+    )
+    rotated = pools["rope"].tile([P, HEADS_PER_BANK, PAIRS, 2], F32, name="rotated")
+    nc.vector.tensor_add(
+        out=rotated[:],
+        in0=cos_part[:].rearrange("p h (j e) -> p h j e", e=2),
+        in1=sin_part[:].rearrange("p e h j -> p h j e"),
+    )
+    queue.dma_start(out=out_columns, in_=rotated[:].rearrange("p h j e -> p (h j e)"))
+
+
+def tile_multiheadflashdiff_pa_k_kernel(
+    tc, x, Wq_words, Wq_scales, Wk_words, Wk_scales, out_0, out_1
+):
+    nc = tc.nc
+    x_rows = x.rearrange("b s e -> (b s) e")
+    q_rows = out_0.rearrange("b s h d -> (b s) (h d)")
+    k_rows = out_1.rearrange("b s h d -> (b s) (h d)")
+
+    with ExitStack() as stack:
+        consts = stack.enter_context(tc.tile_pool(name="consts", bufs=1))
+        pools = {
+            "x": stack.enter_context(tc.tile_pool(name="x", bufs=X_CHUNKS)),
+            "grouped": stack.enter_context(tc.tile_pool(name="grouped", bufs=2)),
+            "w": stack.enter_context(tc.tile_pool(name="w", bufs=W_BUFFERS)),
+            "rope": stack.enter_context(tc.tile_pool(name="rope", bufs=2)),
+            "turned": stack.enter_context(tc.psum_pool(name="turned", bufs=4)),
+        }
+        sums_pool = stack.enter_context(tc.psum_pool(name="sums", bufs=1))
+        stack.enter_context(tc.manual_schedule())
+
+        identity = consts.tile([P, P], F32, name="identity")
+        make_identity(nc, identity[:])
+
+        plane_shape = [P, GROUPS // PLANES_PER_TILE, N]
+        q_planes = consts.tile(plane_shape, U8, name="q_planes", align_bytes=64)
+        k_planes = consts.tile(plane_shape, U8, name="k_planes", align_bytes=64)
+        nc.vector.memset(q_planes[:].bitcast(I32), 0)
+        nc.vector.memset(k_planes[:].bitcast(I32), 0)
+
+        x_codes = consts.tile([P, GROUPS, P], U32, name="x_codes", align_bytes=64)
+        x_scales = consts.tile([P, GROUPS, P], U8, name="x_scales", align_bytes=64)
+        quantise_x(nc, pools, x_rows, identity, x_codes, x_scales)
+        tables = build_rope_tables(nc, consts)
+
+        q_sums = [sums_pool.tile([P, BANK], F32, name="q_sums%d" % b) for b in range(2)]
+        k_sums = [sums_pool.tile([P, BANK], F32, name="k_sums%d" % b) for b in range(2)]
+
+        load_scale_planes(nc, q_planes, Wq_scales)
+        project(nc, pools, Wq_words, q_planes, x_codes, x_scales, q_sums)
+        load_scale_planes(nc, k_planes, Wk_scales)
+        for bank in range(BANKS_PER_WEIGHT):
+            columns = slice(bank * BANK, (bank + 1) * BANK)
+            rotate_and_store(nc, pools, q_sums[bank], tables, q_rows[:, columns], nc.scalar)
+        project(nc, pools, Wk_words, k_planes, x_codes, x_scales, k_sums)
+        for bank in range(BANKS_PER_WEIGHT):
+            columns = slice(bank * BANK, (bank + 1) * BANK)
+            rotate_and_store(nc, pools, k_sums[bank], tables, k_rows[:, columns], nc.sync)

@@ -86,13 +86,14 @@ def quantise_x(nc, pools, x_rows, identity, x_codes, x_scales):
 
 
 def load_scale_planes(nc, planes, scales):
-    for j in range(GROUPS // PLANES_PER_TILE):
-        for quadrant in range(P // QUADRANT):
-            first = quadrant * QUADRANT
-            rows = slice(quadrant * ROWS_PER_QUADRANT, (quadrant + 1) * ROWS_PER_QUADRANT)
-            nc.sync.dma_start(
-                out=planes[first : first + PLANES_PER_TILE * ROWS_PER_QUADRANT, j, :].bitcast(I32),
-                in_=scales[j * PLANES_PER_TILE : (j + 1) * PLANES_PER_TILE, rows, :].bitcast(I32),
+    rows_by_plane = scales.rearrange("(j a) q n -> a q j n", a=PLANES_PER_TILE)
+    for quadrant in range(P // QUADRANT):
+        for r in range(ROWS_PER_QUADRANT):
+            first = quadrant * QUADRANT + r
+            last = first + PLANES_PER_TILE * ROWS_PER_QUADRANT
+            nc.gpsimd.dma_start(
+                out=planes[first:last:ROWS_PER_QUADRANT, :, :].bitcast(F32),
+                in_=rows_by_plane[:, quadrant * ROWS_PER_QUADRANT + r, :, :].bitcast(F32),
             )
 
 
@@ -223,18 +224,18 @@ def tile_multiheadflashdiff_pa_k_kernel(
         k_planes = consts.tile(plane_shape, U8, name="k_planes", align_bytes=64)
         nc.vector.memset(q_planes[:].bitcast(I32), 0)
         nc.vector.memset(k_planes[:].bitcast(I32), 0)
+        tables = build_rope_tables(nc, consts)
+        load_scale_planes(nc, q_planes, Wq_scales)
+        load_scale_planes(nc, k_planes, Wk_scales)
 
         x_codes = consts.tile([P, GROUPS, P], U32, name="x_codes", align_bytes=64)
         x_scales = consts.tile([P, GROUPS, P], U8, name="x_scales", align_bytes=64)
         quantise_x(nc, pools, x_rows, identity, x_codes, x_scales)
-        tables = build_rope_tables(nc, consts)
 
         q_sums = [sums_pool.tile([P, BANK], F32, name="q_sums%d" % b) for b in range(2)]
         k_sums = [sums_pool.tile([P, BANK], F32, name="k_sums%d" % b) for b in range(2)]
 
-        load_scale_planes(nc, q_planes, Wq_scales)
         project(nc, pools, Wq_words, q_planes, x_codes, x_scales, q_sums)
-        load_scale_planes(nc, k_planes, Wk_scales)
         for bank in range(BANKS_PER_WEIGHT):
             columns = slice(bank * BANK, (bank + 1) * BANK)
             rotate_and_store(nc, pools, q_sums[bank], tables, q_rows[:, columns], nc.scalar)

@@ -40,7 +40,7 @@ GROUPS_PER_BANK = 2
 
 W_CHUNK_GROUPS = 2
 W_CHUNKS = GROUPS // W_CHUNK_GROUPS
-W_BUFFERS = 8
+W_BUFFERS = 14
 
 ROUND_MAGIC = 1.5 * 2.0**23
 TWO_PI_HIGH = 6.28125

@@ -39,8 +39,8 @@ WORDS_PER_GROUP = K_PASS // 2
 GROUPS_PER_BANK = 2
 
 W_CHUNK_GROUPS = 2
-W_CHUNKS = GROUPS // W_CHUNK_GROUPS
-W_BUFFERS = 14
+W_BUFFERS = 8
+K_SPLIT_GROUPS = 4
 
 ROUND_MAGIC = 1.5 * 2.0**23
 TWO_PI_HIGH = 6.28125
@@ -85,37 +85,45 @@ def quantise_x(nc, pools, x_rows, identity, x_codes, x_scales):
         )
 
 
-def load_scale_planes(nc, planes, scales):
+def load_scale_planes(queue, word, planes, scales):
     rows_by_plane = scales.rearrange("(j a) q n -> a q j n", a=PLANES_PER_TILE)
     for quadrant in range(P // QUADRANT):
         for r in range(ROWS_PER_QUADRANT):
             first = quadrant * QUADRANT + r
             last = first + PLANES_PER_TILE * ROWS_PER_QUADRANT
-            nc.gpsimd.dma_start(
-                out=planes[first:last:ROWS_PER_QUADRANT, :, :].bitcast(F32),
-                in_=rows_by_plane[:, quadrant * ROWS_PER_QUADRANT + r, :, :].bitcast(F32),
+            queue.dma_start(
+                out=planes[first:last:ROWS_PER_QUADRANT, :, :].bitcast(word),
+                in_=rows_by_plane[:, quadrant * ROWS_PER_QUADRANT + r, :, :].bitcast(word),
             )
 
 
-def project(nc, pools, words, planes, x_codes, x_scales, sums):
+def project(nc, pools, weight, x_codes, x_scales, sums, first_group, end_group, banks):
+    words, planes = weight
     words_by_partition = words.rearrange("g p n t -> p g (n t)")
-    for c in range(W_CHUNKS):
-        w_chunk = pools["w"].tile([P, W_CHUNK_GROUPS, N], U32, name="w_chunk", align_bytes=64)
-        groups = slice(c * W_CHUNK_GROUPS, (c + 1) * W_CHUNK_GROUPS)
-        nc.sync.dma_start(
-            out=w_chunk[:].bitcast(I32), in_=words_by_partition[:, groups, :].bitcast(I32)
+    first_byte = banks[0] * BANK * PACK
+    end_byte = (banks[-1] + 1) * BANK * PACK
+    for first in range(first_group, end_group, W_CHUNK_GROUPS):
+        w_chunk = pools["w"].tile(
+            [P, W_CHUNK_GROUPS, len(banks) * BANK], U32, name="w_chunk", align_bytes=64
         )
-        for bank in range(BANKS_PER_WEIGHT):
-            columns = slice(bank * BANK, (bank + 1) * BANK)
+        nc.sync.dma_start(
+            out=w_chunk[:].bitcast(I32),
+            in_=words_by_partition[
+                :, first : first + W_CHUNK_GROUPS, first_byte:end_byte
+            ].bitcast(I32),
+        )
+        for b, bank in enumerate(banks):
             for i in range(W_CHUNK_GROUPS):
-                g = c * W_CHUNK_GROUPS + i
+                g = first + i
                 plane_offset = ROWS_PER_QUADRANT * (g % PLANES_PER_TILE)
                 nc.tensor.matmul_mx(
                     out=sums[bank][:],
                     lhsT=x_codes[:, g, :].bitcast(FP8X4),
                     lhsT_scale=x_scales[:, g, :],
-                    rhs=w_chunk[:, i, columns].bitcast(FP8X4),
-                    rhs_scale=planes[plane_offset:P, g // PLANES_PER_TILE, columns],
+                    rhs=w_chunk[:, i, b * BANK : (b + 1) * BANK].bitcast(FP8X4),
+                    rhs_scale=planes[
+                        plane_offset:P, g // PLANES_PER_TILE, bank * BANK : (bank + 1) * BANK
+                    ],
                     start=(g == 0),
                     stop=(g == GROUPS - 1),
                 )
@@ -225,8 +233,7 @@ def tile_multiheadflashdiff_pa_k_kernel(
         nc.vector.memset(q_planes[:].bitcast(I32), 0)
         nc.vector.memset(k_planes[:].bitcast(I32), 0)
         tables = build_rope_tables(nc, consts)
-        load_scale_planes(nc, q_planes, Wq_scales)
-        load_scale_planes(nc, k_planes, Wk_scales)
+        load_scale_planes(nc.gpsimd, F32, k_planes, Wk_scales)
 
         x_codes = consts.tile([P, GROUPS, P], U32, name="x_codes", align_bytes=64)
         x_scales = consts.tile([P, GROUPS, P], U8, name="x_scales", align_bytes=64)
@@ -235,11 +242,17 @@ def tile_multiheadflashdiff_pa_k_kernel(
         q_sums = [sums_pool.tile([P, BANK], F32, name="q_sums%d" % b) for b in range(2)]
         k_sums = [sums_pool.tile([P, BANK], F32, name="k_sums%d" % b) for b in range(2)]
 
-        project(nc, pools, Wq_words, q_planes, x_codes, x_scales, q_sums)
-        for bank in range(BANKS_PER_WEIGHT):
+        load_scale_planes(nc.sync, I32, q_planes, Wq_scales)
+        both_banks = list(range(BANKS_PER_WEIGHT))
+        project(nc, pools, (Wq_words, q_planes), x_codes, x_scales, q_sums, 0, GROUPS, both_banks)
+        for bank in both_banks:
             columns = slice(bank * BANK, (bank + 1) * BANK)
             rotate_and_store(nc, pools, q_sums[bank], tables, q_rows[:, columns], nc.scalar)
-        project(nc, pools, Wk_words, k_planes, x_codes, x_scales, k_sums)
-        for bank in range(BANKS_PER_WEIGHT):
+        k_weight = (Wk_words, k_planes)
+        split = GROUPS - K_SPLIT_GROUPS
+        project(nc, pools, k_weight, x_codes, x_scales, k_sums, 0, split, both_banks)
+        for bank in both_banks:
+            project(nc, pools, k_weight, x_codes, x_scales, k_sums, split, GROUPS, [bank])
+        for bank in both_banks:
             columns = slice(bank * BANK, (bank + 1) * BANK)
             rotate_and_store(nc, pools, k_sums[bank], tables, k_rows[:, columns], nc.sync)

@@ -233,7 +233,6 @@ def tile_multiheadflashdiff_pa_k_kernel(
         nc.vector.memset(q_planes[:].bitcast(I32), 0)
         nc.vector.memset(k_planes[:].bitcast(I32), 0)
         tables = build_rope_tables(nc, consts)
-        load_scale_planes(nc.gpsimd, F32, k_planes, Wk_scales)
 
         x_codes = consts.tile([P, GROUPS, P], U32, name="x_codes", align_bytes=64)
         x_scales = consts.tile([P, GROUPS, P], U8, name="x_scales", align_bytes=64)
@@ -243,6 +242,7 @@ def tile_multiheadflashdiff_pa_k_kernel(
         k_sums = [sums_pool.tile([P, BANK], F32, name="k_sums%d" % b) for b in range(2)]
 
         load_scale_planes(nc.sync, I32, q_planes, Wq_scales)
+        load_scale_planes(nc.sync, I32, k_planes, Wk_scales)
         both_banks = list(range(BANKS_PER_WEIGHT))
         project(nc, pools, (Wq_words, q_planes), x_codes, x_scales, q_sums, 0, GROUPS, both_banks)
         for bank in both_banks:

@@ -38,8 +38,9 @@ X_CHUNKS = GROUPS // X_CHUNK_GROUPS
 WORDS_PER_GROUP = K_PASS // 2
 GROUPS_PER_BANK = 2
 
-W_CHUNK_GROUPS = 2
-W_BUFFERS = 8
+W_CHUNK_GROUPS = 4
+W_BUFFERS = 6
+SPLIT_CHUNK_GROUPS = 2
 K_SPLIT_GROUPS = 4
 
 ROUND_MAGIC = 1.5 * 2.0**23
@@ -97,23 +98,21 @@ def load_scale_planes(queue, word, planes, scales):
             )
 
 
-def project(nc, pools, weight, x_codes, x_scales, sums, first_group, end_group, banks):
+def project(nc, pools, weight, x_codes, x_scales, sums, first_group, end_group, banks, chunk):
     words, planes = weight
     words_by_partition = words.rearrange("g p n t -> p g (n t)")
     first_byte = banks[0] * BANK * PACK
     end_byte = (banks[-1] + 1) * BANK * PACK
-    for first in range(first_group, end_group, W_CHUNK_GROUPS):
-        w_chunk = pools["w"].tile(
-            [P, W_CHUNK_GROUPS, len(banks) * BANK], U32, name="w_chunk", align_bytes=64
-        )
+    for first in range(first_group, end_group, chunk):
+        w_chunk = pools["w"].tile([P, chunk, len(banks) * BANK], U32, name="w_chunk", align_bytes=64)
         nc.sync.dma_start(
             out=w_chunk[:].bitcast(I32),
             in_=words_by_partition[
-                :, first : first + W_CHUNK_GROUPS, first_byte:end_byte
+                :, first : first + chunk, first_byte:end_byte
             ].bitcast(I32),
         )
         for b, bank in enumerate(banks):
-            for i in range(W_CHUNK_GROUPS):
+            for i in range(chunk):
                 g = first + i
                 plane_offset = ROWS_PER_QUADRANT * (g % PLANES_PER_TILE)
                 nc.tensor.matmul_mx(
@@ -244,15 +243,20 @@ def tile_multiheadflashdiff_pa_k_kernel(
         load_scale_planes(nc.sync, I32, q_planes, Wq_scales)
         load_scale_planes(nc.sync, I32, k_planes, Wk_scales)
         both_banks = list(range(BANKS_PER_WEIGHT))
-        project(nc, pools, (Wq_words, q_planes), x_codes, x_scales, q_sums, 0, GROUPS, both_banks)
+        q_weight = (Wq_words, q_planes)
+        project(
+            nc, pools, q_weight, x_codes, x_scales, q_sums, 0, GROUPS, both_banks, W_CHUNK_GROUPS
+        )
         for bank in both_banks:
             columns = slice(bank * BANK, (bank + 1) * BANK)
             rotate_and_store(nc, pools, q_sums[bank], tables, q_rows[:, columns], nc.scalar)
         k_weight = (Wk_words, k_planes)
         split = GROUPS - K_SPLIT_GROUPS
-        project(nc, pools, k_weight, x_codes, x_scales, k_sums, 0, split, both_banks)
+        project(nc, pools, k_weight, x_codes, x_scales, k_sums, 0, split, both_banks, W_CHUNK_GROUPS)
         for bank in both_banks:
-            project(nc, pools, k_weight, x_codes, x_scales, k_sums, split, GROUPS, [bank])
+            project(
+                nc, pools, k_weight, x_codes, x_scales, k_sums, split, GROUPS, [bank], SPLIT_CHUNK_GROUPS
+            )
         for bank in both_banks:
             columns = slice(bank * BANK, (bank + 1) * BANK)
             rotate_and_store(nc, pools, k_sums[bank], tables, k_rows[:, columns], nc.sync)

@@ -35,6 +35,7 @@ ROWS_PER_QUADRANT = 4
 
 X_CHUNK_GROUPS = 8
 X_CHUNKS = GROUPS // X_CHUNK_GROUPS
+K_PLANES_BEHIND_X_CHUNK = 1
 WORDS_PER_GROUP = K_PASS // 2
 GROUPS_PER_BANK = 2
 
@@ -50,7 +51,7 @@ TWO_PI_LOW = 2.0 * math.pi - TWO_PI_HIGH
 FLOPS = 2 * P * E * 2 * N
 
 
-def quantise_x(nc, pools, x_rows, identity, x_codes, x_scales):
+def quantise_x(nc, pools, x_rows, identity, x_codes, x_scales, after_chunk):
     for c in range(X_CHUNKS):
         x_chunk = pools["x"].tile([P, X_CHUNK_GROUPS * K_PASS], BF16, name="x_chunk")
         columns = slice(c * X_CHUNK_GROUPS * K_PASS, (c + 1) * X_CHUNK_GROUPS * K_PASS)
@@ -84,11 +85,12 @@ def quantise_x(nc, pools, x_rows, identity, x_codes, x_scales):
             scales=x_scales[:, groups, :].rearrange("p g m -> p (g m)"),
             in_=grouped[:],
         )
+        after_chunk(c)
 
 
-def load_scale_planes(queue, word, planes, scales):
+def load_scale_planes(queue, word, planes, scales, quadrants):
     rows_by_plane = scales.rearrange("(j a) q n -> a q j n", a=PLANES_PER_TILE)
-    for quadrant in range(P // QUADRANT):
+    for quadrant in quadrants:
         for r in range(ROWS_PER_QUADRANT):
             first = quadrant * QUADRANT + r
             last = first + PLANES_PER_TILE * ROWS_PER_QUADRANT
@@ -230,18 +232,22 @@ def tile_multiheadflashdiff_pa_k_kernel(
         q_planes = consts.tile(plane_shape, U8, name="q_planes", align_bytes=64)
         k_planes = consts.tile(plane_shape, U8, name="k_planes", align_bytes=64)
         nc.vector.memset(q_planes[:].bitcast(I32), 0)
-        nc.vector.memset(k_planes[:].bitcast(I32), 0)
         tables = build_rope_tables(nc, consts)
+
+        def start_k_planes_on_gpsimd(x_chunk_index):
+            if x_chunk_index == K_PLANES_BEHIND_X_CHUNK:
+                nc.vector.memset(k_planes[:].bitcast(I32), 0)
+                load_scale_planes(nc.gpsimd, F32, k_planes, Wk_scales, [2, 3])
 
         x_codes = consts.tile([P, GROUPS, P], U32, name="x_codes", align_bytes=64)
         x_scales = consts.tile([P, GROUPS, P], U8, name="x_scales", align_bytes=64)
-        quantise_x(nc, pools, x_rows, identity, x_codes, x_scales)
+        quantise_x(nc, pools, x_rows, identity, x_codes, x_scales, start_k_planes_on_gpsimd)
 
         q_sums = [sums_pool.tile([P, BANK], F32, name="q_sums%d" % b) for b in range(2)]
         k_sums = [sums_pool.tile([P, BANK], F32, name="k_sums%d" % b) for b in range(2)]
 
-        load_scale_planes(nc.sync, I32, q_planes, Wq_scales)
-        load_scale_planes(nc.sync, I32, k_planes, Wk_scales)
+        load_scale_planes(nc.sync, I32, q_planes, Wq_scales, [0, 1, 2, 3])
+        load_scale_planes(nc.sync, I32, k_planes, Wk_scales, [0, 1])
         both_banks = list(range(BANKS_PER_WEIGHT))
         q_weight = (Wq_words, q_planes)
         project(

@@ -177,7 +177,7 @@ def build_rope_tables(nc, consts):
     return cos[:].rearrange("p j e -> p (j e)"), sin_cos[:, 0, :], minus_sin[:]
 
 
-def rotate_and_store(nc, pools, bank_sums, tables, out_columns, queue):
+def rotate(nc, pools, bank_sums, tables):
     cos, sin, minus_sin = tables
     by_head = [P, HEADS_PER_BANK, HEAD_DIM]
     by_pair = [P, HEADS_PER_BANK, PAIRS]
@@ -196,13 +196,13 @@ def rotate_and_store(nc, pools, bank_sums, tables, out_columns, queue):
     nc.vector.tensor_mul(
         out=sin_part[:, 1], in0=partners[:, 0], in1=sin.unsqueeze(1).to_broadcast(by_pair)
     )
-    rotated = pools["rope"].tile([P, HEADS_PER_BANK, PAIRS, 2], F32, name="rotated")
+    rotated = pools["rotated"].tile([P, HEADS_PER_BANK, PAIRS, 2], F32, name="rotated")
     nc.vector.tensor_add(
         out=rotated[:],
         in0=cos_part[:].rearrange("p h (j e) -> p h j e", e=2),
         in1=sin_part[:].rearrange("p e h j -> p h j e"),
     )
-    queue.dma_start(out=out_columns, in_=rotated[:].rearrange("p h j e -> p (h j e)"))
+    return rotated[:].rearrange("p h j e -> p (h j e)")
 
 
 def tile_multiheadflashdiff_pa_k_kernel(
@@ -220,6 +220,7 @@ def tile_multiheadflashdiff_pa_k_kernel(
             "grouped": stack.enter_context(tc.tile_pool(name="grouped", bufs=2)),
             "w": stack.enter_context(tc.tile_pool(name="w", bufs=W_BUFFERS)),
             "rope": stack.enter_context(tc.tile_pool(name="rope", bufs=2)),
+            "rotated": stack.enter_context(tc.tile_pool(name="rotated", bufs=2 * BANKS_PER_WEIGHT)),
             "turned": stack.enter_context(tc.psum_pool(name="turned", bufs=4)),
         }
         sums_pool = stack.enter_context(tc.psum_pool(name="sums", bufs=1))
@@ -253,9 +254,7 @@ def tile_multiheadflashdiff_pa_k_kernel(
         project(
             nc, pools, q_weight, x_codes, x_scales, q_sums, 0, GROUPS, both_banks, W_CHUNK_GROUPS
         )
-        for bank in both_banks:
-            columns = slice(bank * BANK, (bank + 1) * BANK)
-            rotate_and_store(nc, pools, q_sums[bank], tables, q_rows[:, columns], nc.scalar)
+        q_rotated = [rotate(nc, pools, q_sums[bank], tables) for bank in both_banks]
         k_weight = (Wk_words, k_planes)
         split = GROUPS - K_SPLIT_GROUPS
         project(nc, pools, k_weight, x_codes, x_scales, k_sums, 0, split, both_banks, W_CHUNK_GROUPS)
@@ -264,5 +263,7 @@ def tile_multiheadflashdiff_pa_k_kernel(
                 nc, pools, k_weight, x_codes, x_scales, k_sums, split, GROUPS, [bank], SPLIT_CHUNK_GROUPS
             )
         for bank in both_banks:
-            columns = slice(bank * BANK, (bank + 1) * BANK)
-            rotate_and_store(nc, pools, k_sums[bank], tables, k_rows[:, columns], nc.sync)
+            nc.sync.dma_start(out=q_rows[:, bank * BANK : (bank + 1) * BANK], in_=q_rotated[bank])
+        for bank in both_banks:
+            k_rotated = rotate(nc, pools, k_sums[bank], tables)
+            nc.sync.dma_start(out=k_rows[:, bank * BANK : (bank + 1) * BANK], in_=k_rotated)

@@ -35,7 +35,7 @@ ROWS_PER_QUADRANT = 4
 
 X_CHUNK_GROUPS = 8
 X_CHUNKS = GROUPS // X_CHUNK_GROUPS
-K_PLANES_BEHIND_X_CHUNK = 1
+K_PLANES_BEHIND_X_CHUNK = 0
 WORDS_PER_GROUP = K_PASS // 2
 GROUPS_PER_BANK = 2
 

@@ -247,7 +247,7 @@ def tile_multiheadflashdiff_pa_k_kernel(
         q_sums = [sums_pool.tile([P, BANK], F32, name="q_sums%d" % b) for b in range(2)]
         k_sums = [sums_pool.tile([P, BANK], F32, name="k_sums%d" % b) for b in range(2)]
 
-        load_scale_planes(nc.sync, I32, q_planes, Wq_scales, [0, 1, 2, 3])
+        load_scale_planes(nc.sync, I32, q_planes, Wq_scales, [2, 3, 0, 1])
         load_scale_planes(nc.sync, I32, k_planes, Wk_scales, [0, 1])
         both_banks = list(range(BANKS_PER_WEIGHT))
         q_weight = (Wq_words, q_planes)

@@ -27,7 +27,6 @@ K_PASS = P * PACK
 GROUPS = E // K_PASS
 BANK = 512
 BANKS_PER_WEIGHT = N // BANK
-HEADS_PER_BANK = BANK // HEAD_DIM
 
 PLANES_PER_TILE = 4
 QUADRANT = 32
@@ -41,8 +40,10 @@ GROUPS_PER_BANK = 2
 
 W_CHUNK_GROUPS = 4
 W_BUFFERS = 6
-SPLIT_CHUNK_GROUPS = 2
-K_SPLIT_GROUPS = 4
+Q_PIECE_WIDTHS = (BANK, BANK)
+K_PIECE_WIDTHS = (BANK, BANK // 2, BANK // 2)
+K_FIRST_PIECE_APART = 24
+K_NARROW_PIECES_APART = 28
 
 ROUND_MAGIC = 1.5 * 2.0**23
 TWO_PI_HIGH = 6.28125
@@ -100,31 +101,32 @@ def load_scale_planes(queue, word, planes, scales, quadrants):
             )
 
 
-def project(nc, pools, weight, x_codes, x_scales, sums, first_group, end_group, banks, chunk):
+def project(nc, pools, weight, x_codes, x_scales, pieces, first_group, end_group):
     words, planes = weight
     words_by_partition = words.rearrange("g p n t -> p g (n t)")
-    first_byte = banks[0] * BANK * PACK
-    end_byte = (banks[-1] + 1) * BANK * PACK
-    for first in range(first_group, end_group, chunk):
-        w_chunk = pools["w"].tile([P, chunk, len(banks) * BANK], U32, name="w_chunk", align_bytes=64)
+    first_column = pieces[0][1]
+    end_column = pieces[-1][1] + pieces[-1][2]
+    for first in range(first_group, end_group, W_CHUNK_GROUPS):
+        w_chunk = pools["w"].tile(
+            [P, W_CHUNK_GROUPS, end_column - first_column], U32, name="w_chunk", align_bytes=64
+        )
         nc.sync.dma_start(
             out=w_chunk[:].bitcast(I32),
             in_=words_by_partition[
-                :, first : first + chunk, first_byte:end_byte
+                :, first : first + W_CHUNK_GROUPS, first_column * PACK : end_column * PACK
             ].bitcast(I32),
         )
-        for b, bank in enumerate(banks):
-            for i in range(chunk):
+        for sums, column, width in pieces:
+            for i in range(W_CHUNK_GROUPS):
                 g = first + i
                 plane_offset = ROWS_PER_QUADRANT * (g % PLANES_PER_TILE)
+                in_chunk = column - first_column
                 nc.tensor.matmul_mx(
-                    out=sums[bank][:],
+                    out=sums[:],
                     lhsT=x_codes[:, g, :].bitcast(FP8X4),
                     lhsT_scale=x_scales[:, g, :],
-                    rhs=w_chunk[:, i, b * BANK : (b + 1) * BANK].bitcast(FP8X4),
-                    rhs_scale=planes[
-                        plane_offset:P, g // PLANES_PER_TILE, bank * BANK : (bank + 1) * BANK
-                    ],
+                    rhs=w_chunk[:, i, in_chunk : in_chunk + width].bitcast(FP8X4),
+                    rhs_scale=planes[plane_offset:P, g // PLANES_PER_TILE, column : column + width],
                     start=(g == 0),
                     stop=(g == GROUPS - 1),
                 )
@@ -177,10 +179,12 @@ def build_rope_tables(nc, consts):
     return cos[:].rearrange("p j e -> p (j e)"), sin_cos[:, 0, :], minus_sin[:]
 
 
-def rotate(nc, pools, bank_sums, tables):
+def rotate(nc, pools, piece, tables):
     cos, sin, minus_sin = tables
-    by_head = [P, HEADS_PER_BANK, HEAD_DIM]
-    by_pair = [P, HEADS_PER_BANK, PAIRS]
+    bank_sums = piece[0]
+    heads = piece[2] // HEAD_DIM
+    by_head = [P, heads, HEAD_DIM]
+    by_pair = [P, heads, PAIRS]
 
     cos_part = pools["rope"].tile(by_head, F32, name="cos_part")
     nc.vector.tensor_mul(
@@ -189,20 +193,28 @@ def rotate(nc, pools, bank_sums, tables):
         in1=cos.unsqueeze(1).to_broadcast(by_head),
     )
     partners = bank_sums[:].rearrange("p (h j e) -> p e h j", j=PAIRS, e=2)
-    sin_part = pools["rope"].tile([P, 2, HEADS_PER_BANK, PAIRS], F32, name="sin_part")
+    sin_part = pools["rope"].tile([P, 2, heads, PAIRS], F32, name="sin_part")
     nc.vector.tensor_mul(
         out=sin_part[:, 0], in0=partners[:, 1], in1=minus_sin.unsqueeze(1).to_broadcast(by_pair)
     )
     nc.vector.tensor_mul(
         out=sin_part[:, 1], in0=partners[:, 0], in1=sin.unsqueeze(1).to_broadcast(by_pair)
     )
-    rotated = pools["rotated"].tile([P, HEADS_PER_BANK, PAIRS, 2], F32, name="rotated")
+    rotated = pools["rotated"].tile([P, heads, PAIRS, 2], F32, name="rotated")
     nc.vector.tensor_add(
         out=rotated[:],
         in0=cos_part[:].rearrange("p h (j e) -> p h j e", e=2),
         in1=sin_part[:].rearrange("p e h j -> p h j e"),
     )
     return rotated[:].rearrange("p h j e -> p (h j e)")
+
+
+def open_pieces(sums_pool, name, widths):
+    pieces = []
+    for i, width in enumerate(widths):
+        sums = sums_pool.tile([P, width], F32, name=name % i)
+        pieces.append((sums, sum(widths[:i]), width))
+    return pieces
 
 
 def tile_multiheadflashdiff_pa_k_kernel(
@@ -220,8 +232,10 @@ def tile_multiheadflashdiff_pa_k_kernel(
             "grouped": stack.enter_context(tc.tile_pool(name="grouped", bufs=2)),
             "w": stack.enter_context(tc.tile_pool(name="w", bufs=W_BUFFERS)),
             "rope": stack.enter_context(tc.tile_pool(name="rope", bufs=2)),
-            "rotated": stack.enter_context(tc.tile_pool(name="rotated", bufs=2 * BANKS_PER_WEIGHT)),
-            "turned": stack.enter_context(tc.psum_pool(name="turned", bufs=4)),
+            "rotated": stack.enter_context(
+                tc.tile_pool(name="rotated", bufs=len(Q_PIECE_WIDTHS) + len(K_PIECE_WIDTHS))
+            ),
+            "turned": stack.enter_context(tc.psum_pool(name="turned", bufs=3)),
         }
         sums_pool = stack.enter_context(tc.psum_pool(name="sums", bufs=1))
         stack.enter_context(tc.manual_schedule())
@@ -244,26 +258,23 @@ def tile_multiheadflashdiff_pa_k_kernel(
         x_scales = consts.tile([P, GROUPS, P], U8, name="x_scales", align_bytes=64)
         quantise_x(nc, pools, x_rows, identity, x_codes, x_scales, start_k_planes_on_gpsimd)
 
-        q_sums = [sums_pool.tile([P, BANK], F32, name="q_sums%d" % b) for b in range(2)]
-        k_sums = [sums_pool.tile([P, BANK], F32, name="k_sums%d" % b) for b in range(2)]
+        q_pieces = open_pieces(sums_pool, "q_sums%d", Q_PIECE_WIDTHS)
+        k_pieces = open_pieces(sums_pool, "k_sums%d", K_PIECE_WIDTHS)
 
         load_scale_planes(nc.sync, I32, q_planes, Wq_scales, [2, 3, 0, 1])
         load_scale_planes(nc.sync, I32, k_planes, Wk_scales, [0, 1])
-        both_banks = list(range(BANKS_PER_WEIGHT))
-        q_weight = (Wq_words, q_planes)
-        project(
-            nc, pools, q_weight, x_codes, x_scales, q_sums, 0, GROUPS, both_banks, W_CHUNK_GROUPS
-        )
-        q_rotated = [rotate(nc, pools, q_sums[bank], tables) for bank in both_banks]
+        project(nc, pools, (Wq_words, q_planes), x_codes, x_scales, q_pieces, 0, GROUPS)
+        q_rotated = [rotate(nc, pools, piece, tables) for piece in q_pieces]
         k_weight = (Wk_words, k_planes)
-        split = GROUPS - K_SPLIT_GROUPS
-        project(nc, pools, k_weight, x_codes, x_scales, k_sums, 0, split, both_banks, W_CHUNK_GROUPS)
-        for bank in both_banks:
-            project(
-                nc, pools, k_weight, x_codes, x_scales, k_sums, split, GROUPS, [bank], SPLIT_CHUNK_GROUPS
-            )
-        for bank in both_banks:
-            nc.sync.dma_start(out=q_rows[:, bank * BANK : (bank + 1) * BANK], in_=q_rotated[bank])
-        for bank in both_banks:
-            k_rotated = rotate(nc, pools, k_sums[bank], tables)
-            nc.sync.dma_start(out=k_rows[:, bank * BANK : (bank + 1) * BANK], in_=k_rotated)
+        project(nc, pools, k_weight, x_codes, x_scales, k_pieces, 0, K_FIRST_PIECE_APART)
+        project(nc, pools, k_weight, x_codes, x_scales, k_pieces[:1], K_FIRST_PIECE_APART, GROUPS)
+        project(
+            nc, pools, k_weight, x_codes, x_scales, k_pieces[1:], K_FIRST_PIECE_APART, K_NARROW_PIECES_APART
+        )
+        for piece in k_pieces[1:]:
+            project(nc, pools, k_weight, x_codes, x_scales, [piece], K_NARROW_PIECES_APART, GROUPS)
+        for piece, rotated in zip(q_pieces, q_rotated):
+            nc.sync.dma_start(out=q_rows[:, piece[1] : piece[1] + piece[2]], in_=rotated)
+        for piece in k_pieces:
+            rotated = rotate(nc, pools, piece, tables)
+            nc.sync.dma_start(out=k_rows[:, piece[1] : piece[1] + piece[2]], in_=rotated)

import math
from contextlib import ExitStack

import concourse.mybir as mybir
from concourse.masks import make_identity

F32 = mybir.dt.float32
BF16 = mybir.dt.bfloat16
I32 = mybir.dt.int32
U32 = mybir.dt.uint32
U8 = mybir.dt.uint8
FP8X4 = mybir.dt.float8_e4m3fn_x4
ALU = mybir.AluOpType
ACT = mybir.ActivationFunctionType

P = 128
POSITIONS = 64
E = 16384
HEAD_DIM = 64
PAIRS = HEAD_DIM // 2
DOUBLINGS = 5
N = 1024
ROPE_BASE = 10000.0

PACK = 4
K_PASS = P * PACK
GROUPS = E // K_PASS
BANK = 512
BANKS_PER_WEIGHT = N // BANK

PLANES_PER_TILE = 4
QUADRANT = 32
ROWS_PER_QUADRANT = 4

X_CHUNK_GROUPS = 8
X_CHUNKS = GROUPS // X_CHUNK_GROUPS
K_PLANES_BEHIND_X_CHUNK = 0
WORDS_PER_GROUP = K_PASS // 2
GROUPS_PER_BANK = 2

W_CHUNK_GROUPS = 4
W_BUFFERS = 6
Q_PIECE_WIDTHS = (BANK, BANK)
K_PIECE_WIDTHS = (BANK, BANK // 2, BANK // 2)
K_FIRST_PIECE_APART = 24
K_NARROW_PIECES_APART = 28

ROUND_MAGIC = 1.5 * 2.0**23
TWO_PI_HIGH = 6.28125
TWO_PI_LOW = 2.0 * math.pi - TWO_PI_HIGH

FLOPS = 2 * P * E * 2 * N


def quantise_x(nc, pools, x_rows, identity, x_codes, x_scales, after_chunk):
    for c in range(X_CHUNKS):
        x_chunk = pools["x"].tile([P, X_CHUNK_GROUPS * K_PASS], BF16, name="x_chunk")
        columns = slice(c * X_CHUNK_GROUPS * K_PASS, (c + 1) * X_CHUNK_GROUPS * K_PASS)
        nc.sync.dma_start(out=x_chunk[:], in_=x_rows[:, columns])
        x_words = x_chunk[:].bitcast(F32)

        grouped = pools["grouped"].tile(
            [P, X_CHUNK_GROUPS * K_PASS], BF16, name="grouped", align_bytes=64
        )
        grouped_words = grouped[:].bitcast(F32)
        for b in range(X_CHUNK_GROUPS // GROUPS_PER_BANK):
            turned = pools["turned"].tile([P, GROUPS_PER_BANK * 2, P], F32, name="turned")
            for i in range(GROUPS_PER_BANK):
                first = (b * GROUPS_PER_BANK + i) * WORDS_PER_GROUP
                for u in range(2):
                    nc.tensor.transpose(
                        turned[:, 2 * i + u, :],
                        x_words[:, first + u : first + WORDS_PER_GROUP : 2],
                        identity[:],
                    )
            copy = nc.vector.tensor_copy if b % 2 == 0 else nc.scalar.copy
            copy(
                out=grouped_words[:, b * BANK : (b + 1) * BANK].rearrange(
                    "p (g m u) -> p g m u", g=GROUPS_PER_BANK, u=2
                ),
                in_=turned[:].rearrange("p (g u) m -> p g m u", u=2),
            )
        groups = slice(c * X_CHUNK_GROUPS, (c + 1) * X_CHUNK_GROUPS)
        nc.vector.quantize_mx(
            out=x_codes[:, groups, :].rearrange("p g m -> p (g m)").bitcast(FP8X4),
            scales=x_scales[:, groups, :].rearrange("p g m -> p (g m)"),
            in_=grouped[:],
        )
        after_chunk(c)


def load_scale_planes(queue, word, planes, scales, quadrants):
    rows_by_plane = scales.rearrange("(j a) q n -> a q j n", a=PLANES_PER_TILE)
    for quadrant in quadrants:
        for r in range(ROWS_PER_QUADRANT):
            first = quadrant * QUADRANT + r
            last = first + PLANES_PER_TILE * ROWS_PER_QUADRANT
            queue.dma_start(
                out=planes[first:last:ROWS_PER_QUADRANT, :, :].bitcast(word),
                in_=rows_by_plane[:, quadrant * ROWS_PER_QUADRANT + r, :, :].bitcast(word),
            )


def project(nc, pools, weight, x_codes, x_scales, pieces, first_group, end_group):
    words, planes = weight
    words_by_partition = words.rearrange("g p n t -> p g (n t)")
    first_column = pieces[0][1]
    end_column = pieces[-1][1] + pieces[-1][2]
    for first in range(first_group, end_group, W_CHUNK_GROUPS):
        w_chunk = pools["w"].tile(
            [P, W_CHUNK_GROUPS, end_column - first_column], U32, name="w_chunk", align_bytes=64
        )
        nc.sync.dma_start(
            out=w_chunk[:].bitcast(I32),
            in_=words_by_partition[
                :, first : first + W_CHUNK_GROUPS, first_column * PACK : end_column * PACK
            ].bitcast(I32),
        )
        for sums, column, width in pieces:
            for i in range(W_CHUNK_GROUPS):
                g = first + i
                plane_offset = ROWS_PER_QUADRANT * (g % PLANES_PER_TILE)
                in_chunk = column - first_column
                nc.tensor.matmul_mx(
                    out=sums[:],
                    lhsT=x_codes[:, g, :].bitcast(FP8X4),
                    lhsT_scale=x_scales[:, g, :],
                    rhs=w_chunk[:, i, in_chunk : in_chunk + width].bitcast(FP8X4),
                    rhs_scale=planes[plane_offset:P, g // PLANES_PER_TILE, column : column + width],
                    start=(g == 0),
                    stop=(g == GROUPS - 1),
                )


def build_rope_tables(nc, consts):
    position_int = consts.tile([P, 1], I32, name="position_int")
    nc.gpsimd.iota(position_int[:], pattern=[[1, 1]], base=0, channel_multiplier=1)
    nc.vector.tensor_single_scalar(
        out=position_int[:], in_=position_int[:], scalar=POSITIONS - 1, op=ALU.bitwise_and
    )
    position = consts.tile([P, 1], F32, name="position")
    nc.vector.tensor_copy(out=position[:], in_=position_int[:])

    frequency = consts.tile([P, PAIRS], F32, name="frequency")
    nc.vector.memset(frequency[:, 0:1], 1.0)
    for doubling in range(DOUBLINGS):
        width = 2**doubling
        nc.vector.tensor_scalar_mul(
            out=frequency[:, width : 2 * width],
            in0=frequency[:, 0:width],
            scalar1=ROPE_BASE ** (-2.0 * width / HEAD_DIM),
        )

    angle = consts.tile([P, 2, PAIRS], F32, name="angle")
    nc.vector.tensor_scalar_mul(out=angle[:, 0, :], in0=frequency[:], scalar1=position[:, 0:1])
    nc.vector.tensor_scalar_add(out=angle[:, 1, :], in0=angle[:, 0, :], scalar1=math.pi / 2.0)

    turns = consts.tile([P, 2, PAIRS], F32, name="turns")
    nc.vector.tensor_scalar(
        out=turns[:],
        in0=angle[:],
        scalar1=1.0 / (2.0 * math.pi),
        scalar2=ROUND_MAGIC,
        op0=ALU.mult,
        op1=ALU.add,
    )
    nc.vector.tensor_scalar_sub(out=turns[:], in0=turns[:], scalar1=ROUND_MAGIC)
    for part in (TWO_PI_HIGH, TWO_PI_LOW):
        nc.vector.scalar_tensor_tensor(
            out=angle[:], in0=turns[:], scalar=-part, in1=angle[:], op0=ALU.mult, op1=ALU.add
        )
    sin_cos = consts.tile([P, 2, PAIRS], F32, name="sin_cos")
    nc.scalar.activation(out=sin_cos[:], in_=angle[:], func=ACT.Sin)

    cos = consts.tile([P, PAIRS, 2], F32, name="cos")
    nc.vector.tensor_copy(out=cos[:], in_=sin_cos[:, 1, :].unsqueeze(2).to_broadcast([P, PAIRS, 2]))
    minus_sin = consts.tile([P, PAIRS], F32, name="minus_sin")
    nc.vector.tensor_scalar_mul(out=minus_sin[:], in0=sin_cos[:, 0, :], scalar1=-1.0)
    return cos[:].rearrange("p j e -> p (j e)"), sin_cos[:, 0, :], minus_sin[:]


def rotate(nc, pools, piece, tables):
    cos, sin, minus_sin = tables
    bank_sums = piece[0]
    heads = piece[2] // HEAD_DIM
    by_head = [P, heads, HEAD_DIM]
    by_pair = [P, heads, PAIRS]

    cos_part = pools["rope"].tile(by_head, F32, name="cos_part")
    nc.vector.tensor_mul(
        out=cos_part[:],
        in0=bank_sums[:].rearrange("p (h d) -> p h d", d=HEAD_DIM),
        in1=cos.unsqueeze(1).to_broadcast(by_head),
    )
    partners = bank_sums[:].rearrange("p (h j e) -> p e h j", j=PAIRS, e=2)
    sin_part = pools["rope"].tile([P, 2, heads, PAIRS], F32, name="sin_part")
    nc.vector.tensor_mul(
        out=sin_part[:, 0], in0=partners[:, 1], in1=minus_sin.unsqueeze(1).to_broadcast(by_pair)
    )
    nc.vector.tensor_mul(
        out=sin_part[:, 1], in0=partners[:, 0], in1=sin.unsqueeze(1).to_broadcast(by_pair)
    )
    rotated = pools["rotated"].tile([P, heads, PAIRS, 2], F32, name="rotated")
    nc.vector.tensor_add(
        out=rotated[:],
        in0=cos_part[:].rearrange("p h (j e) -> p h j e", e=2),
        in1=sin_part[:].rearrange("p e h j -> p h j e"),
    )
    return rotated[:].rearrange("p h j e -> p (h j e)")


def open_pieces(sums_pool, name, widths):
    pieces = []
    for i, width in enumerate(widths):
        sums = sums_pool.tile([P, width], F32, name=name % i)
        pieces.append((sums, sum(widths[:i]), width))
    return pieces


def tile_multiheadflashdiff_pa_k_kernel(
    tc, x, Wq_words, Wq_scales, Wk_words, Wk_scales, out_0, out_1
):
    nc = tc.nc
    x_rows = x.rearrange("b s e -> (b s) e")
    q_rows = out_0.rearrange("b s h d -> (b s) (h d)")
    k_rows = out_1.rearrange("b s h d -> (b s) (h d)")

    with ExitStack() as stack:
        consts = stack.enter_context(tc.tile_pool(name="consts", bufs=1))
        pools = {
            "x": stack.enter_context(tc.tile_pool(name="x", bufs=X_CHUNKS)),
            "grouped": stack.enter_context(tc.tile_pool(name="grouped", bufs=2)),
            "w": stack.enter_context(tc.tile_pool(name="w", bufs=W_BUFFERS)),
            "rope": stack.enter_context(tc.tile_pool(name="rope", bufs=2)),
            "rotated": stack.enter_context(
                tc.tile_pool(name="rotated", bufs=len(Q_PIECE_WIDTHS) + len(K_PIECE_WIDTHS))
            ),
            "turned": stack.enter_context(tc.psum_pool(name="turned", bufs=3)),
        }
        sums_pool = stack.enter_context(tc.psum_pool(name="sums", bufs=1))
        stack.enter_context(tc.manual_schedule())

        identity = consts.tile([P, P], F32, name="identity")
        make_identity(nc, identity[:])

        plane_shape = [P, GROUPS // PLANES_PER_TILE, N]
        q_planes = consts.tile(plane_shape, U8, name="q_planes", align_bytes=64)
        k_planes = consts.tile(plane_shape, U8, name="k_planes", align_bytes=64)
        nc.vector.memset(q_planes[:].bitcast(I32), 0)
        tables = build_rope_tables(nc, consts)

        def start_k_planes_on_gpsimd(x_chunk_index):
            if x_chunk_index == K_PLANES_BEHIND_X_CHUNK:
                nc.vector.memset(k_planes[:].bitcast(I32), 0)
                load_scale_planes(nc.gpsimd, F32, k_planes, Wk_scales, [2, 3])

        x_codes = consts.tile([P, GROUPS, P], U32, name="x_codes", align_bytes=64)
        x_scales = consts.tile([P, GROUPS, P], U8, name="x_scales", align_bytes=64)
        quantise_x(nc, pools, x_rows, identity, x_codes, x_scales, start_k_planes_on_gpsimd)

        q_pieces = open_pieces(sums_pool, "q_sums%d", Q_PIECE_WIDTHS)
        k_pieces = open_pieces(sums_pool, "k_sums%d", K_PIECE_WIDTHS)

        load_scale_planes(nc.sync, I32, q_planes, Wq_scales, [2, 3, 0, 1])
        load_scale_planes(nc.sync, I32, k_planes, Wk_scales, [0, 1])
        project(nc, pools, (Wq_words, q_planes), x_codes, x_scales, q_pieces, 0, GROUPS)
        q_rotated = [rotate(nc, pools, piece, tables) for piece in q_pieces]
        k_weight = (Wk_words, k_planes)
        project(nc, pools, k_weight, x_codes, x_scales, k_pieces, 0, K_FIRST_PIECE_APART)
        project(nc, pools, k_weight, x_codes, x_scales, k_pieces[:1], K_FIRST_PIECE_APART, GROUPS)
        project(
            nc, pools, k_weight, x_codes, x_scales, k_pieces[1:], K_FIRST_PIECE_APART, K_NARROW_PIECES_APART
        )
        for piece in k_pieces[1:]:
            project(nc, pools, k_weight, x_codes, x_scales, [piece], K_NARROW_PIECES_APART, GROUPS)
        for piece, rotated in zip(q_pieces, q_rotated):
            nc.sync.dma_start(out=q_rows[:, piece[1] : piece[1] + piece[2]], in_=rotated)
        for piece in k_pieces:
            rotated = rotate(nc, pools, piece, tables)
            nc.sync.dma_start(out=k_rows[:, piece[1] : piece[1] + piece[2]], in_=rotated)
